import numpy as np
import ml_dtypes


def mxq(x, axis, fmt="e4m3"):
    dtype, down = {"e4m3": (ml_dtypes.float8_e4m3fn, 7), "e5m2": (ml_dtypes.float8_e5m2, 14)}[fmt]
    v = np.moveaxis(np.asarray(x, np.float32).astype(ml_dtypes.bfloat16).astype(np.float64), axis, -1)
    blocks = v.reshape(v.shape[:-1] + (-1, 32))
    amax = np.abs(blocks).max(-1, keepdims=True)
    byte = np.maximum(np.where(amax > 0, np.frexp(amax)[1] - 1 + 127, 0) - down, 1)
    scale = np.exp2(byte - 127.0)
    codes = (blocks / scale).astype(np.float32).astype(dtype).astype(np.float64)
    return np.moveaxis((codes * scale).reshape(v.shape), -1, axis)


WIDE = False


def mx_kscale(k):
    if not WIDE:
        return np.ones(k)
    levels = np.array([20, -20, 10, -10, 0])
    a = np.random.permutation(np.resize(levels, k // 512 * 4)).reshape(k // 512, 4)
    idx = np.arange(k)
    return np.exp2(a[idx // 512, idx % 128 // 32])


BF16 = ml_dtypes.bfloat16


def bf(x):
    return np.asarray(x, np.float32).astype(BF16)


def f64(x):
    return np.asarray(x).astype(np.float64)


B, S, I, O = 1, 2048, 1024, 2048
T = B * S


def setup_inputs():
    s = mx_kscale(T).reshape(B, S, 1)
    sc = float(np.exp2(-np.random.randint(4, 7)))
    x = np.random.standard_normal((B, S, I)) * s
    u = np.clip(np.round(np.random.standard_normal((O, I)) * 0.4 * 2.0) / 2.0, -1.0, 1.0) + 0.0
    weight = u * sc
    g = np.random.standard_normal((B, S, O)) * np.exp2(np.random.randint(-12, 1, (B, S, 1))) / s
    return {"x": bf(x), "weight": bf(weight), "scale": bf(np.array([sc])), "grad_out": bf(g)}


def reference(x, weight, scale, grad_out):
    xq = mxq(f64(x).reshape(T, I), 0, "e4m3")
    gq = mxq(f64(grad_out).reshape(T, O), 0, "e5m2")
    return gq.T @ xq

@@ -1,0 +1,196 @@
+from contextlib import ExitStack
+
+import concourse.mybir as mybir
+
+FLOPS = 2 * 2048 * 2048 * 1024
+BYTES = 2 * 2048 * 1024 + 2 * 2048 * 2048 + 4 * 2048 * 1024
+
+BF16 = mybir.dt.bfloat16
+F32 = mybir.dt.float32
+U32 = mybir.dt.uint32
+U8 = mybir.dt.uint8
+E4M3 = mybir.dt.float8_e4m3fn_x4
+E5M2 = mybir.dt.float8_e5m2_x4
+
+P = 128
+PACK = 4
+PASSES = 4
+UNIT = 512
+BLOCKS = 4
+TILES = 4
+S_COLS = (256, 0, 192, 192)
+PINNED = True
+
+
+def regroup(copy, grouped, source, col0, lo, hi):
+    copy(
+        out=grouped[:, lo:hi, :].rearrange("p (c i) t -> p c t i", i=4),
+        in_=source[:, :, col0 + lo : col0 + hi].rearrange("p t (c i) -> p c t i", i=4),
+    )
+
+
+def tile_primallinear_kernel(tc, x, weight, scale, grad_out, out):
+    nc = tc.nc
+    xv = x.rearrange("b (c p j) i -> (b c) p j i", p=P, j=PACK)
+    gv = grad_out.rearrange("b (c p j) o -> (b c) p j o", p=P, j=PACK)
+    with ExitStack() as ctx:
+        raw = ctx.enter_context(tc.tile_pool(name="raw", bufs=1))
+        keep = ctx.enter_context(tc.tile_pool(name="keep", bufs=1))
+        grp = ctx.enter_context(tc.tile_pool(name="grp", bufs=6))
+        stage = ctx.enter_context(tc.tile_pool(name="stage", bufs=8))
+        psum = ctx.enter_context(tc.psum_pool(name="psum", bufs=1))
+        if PINNED:
+            ctx.enter_context(tc.manual_schedule())
+
+        x_raw = []
+        g_raw = {}
+
+        def load_g(b, c):
+            t = raw.tile([P, PACK, UNIT], BF16, name="graw%d_%d" % (b, c))
+            nc.sync.dma_start(out=t[:], in_=gv[c, :, :, b * UNIT : (b + 1) * UNIT])
+            g_raw[(b, c)] = t
+
+        for c in range(PASSES):
+            t = raw.tile([P, PACK, 2 * UNIT], BF16, name="xraw%d" % c)
+            nc.sync.dma_start(out=t[:], in_=xv[c, :, :, :])
+            x_raw.append(t)
+            load_g(0, c)
+        for b in range(1, BLOCKS):
+            for c in range(PASSES):
+                load_g(b, c)
+
+        x_q = {}
+        g_q = {}
+        g_grouped = {}
+
+        def new_grouped():
+            t = grp.tile([P, UNIT, PACK], BF16, name="grouped", align_bytes=64)
+            return t
+
+        def quantise(grouped, fmt, label):
+            codes = keep.tile([P, UNIT], U32, name="codes_" + label, align_bytes=64)
+            scales = keep.tile([P, UNIT], U8, name="scales_" + label, align_bytes=64)
+            nc.vector.quantize_mx(
+                out=codes[:].bitcast(fmt),
+                scales=scales[:],
+                in_=grouped[:].rearrange("p w t -> p (w t)"),
+            )
+            return codes, scales
+
+        def g_tile(b, c):
+            if (b, c) not in g_grouped:
+                g_grouped[(b, c)] = new_grouped()
+            return g_grouped[(b, c)]
+
+        def g_copy_vector(b, c):
+            regroup(nc.vector.tensor_copy, g_tile(b, c), g_raw[(b, c)], 0, 0, UNIT - S_COLS[b])
+
+        def g_copy_scalar(b, c):
+            if S_COLS[b] > 0:
+                regroup(nc.scalar.copy, g_tile(b, c), g_raw[(b, c)], 0, UNIT - S_COLS[b], UNIT)
+
+        def g_quantise(b, c):
+            g_q[(b, c)] = quantise(g_tile(b, c), E5M2, "g%d_%d" % (b, c))
+
+        acc = {}
+
+        def mx_pass(t, h, c):
+            if c == 0:
+                bank = (t % TILES) * 2 + h
+                acc[(t, h)] = psum.tile([P, UNIT], F32, name="acc%d" % bank)
+            codes, scales = g_q[(t // TILES, c)]
+            m0 = (t % TILES) * P
+            xc, xs = x_q[(h, c)]
+            nc.tensor.matmul_mx(
+                out=acc[(t, h)][:],
+                lhsT=codes[:, m0 : m0 + P].bitcast(E5M2),
+                lhsT_scale=scales[:, m0 : m0 + P],
+                rhs=xc[:].bitcast(E4M3),
+                rhs_scale=xs[:],
+                start=(c == 0),
+                stop=(c == PASSES - 1),
+            )
+
+        staged = {}
+
+        def evacuate(t, h, copy):
+            if t not in staged:
+                staged[t] = stage.tile([P, 2 * UNIT], F32, name="staged")
+            copy(out=staged[t][:, h * UNIT : (h + 1) * UNIT], in_=acc[(t, h)][:])
+
+        def store(t):
+            nc.sync.dma_start(out=out[t * P : (t + 1) * P, :], in_=staged[t][:])
+
+        def store_half(t, h):
+            nc.sync.dma_start(
+                out=out[t * P : (t + 1) * P, h * UNIT : (h + 1) * UNIT],
+                in_=staged[t][:, h * UNIT : (h + 1) * UNIT],
+            )
+
+        def vector_block(b):
+            g_copy_vector(b, 0)
+            g_copy_vector(b, 1)
+            g_quantise(b, 0)
+            g_copy_vector(b, 2)
+            g_quantise(b, 1)
+            g_copy_vector(b, 3)
+            g_quantise(b, 2)
+            g_quantise(b, 3)
+
+        for c in range(PASSES):
+            lo = new_grouped()
+            hi = new_grouped()
+            regroup(nc.vector.tensor_copy, lo, x_raw[c], 0, 0, UNIT)
+            regroup(nc.scalar.copy, hi, x_raw[c], UNIT, 0, UNIT)
+            g_copy_vector(0, c)
+            g_copy_scalar(0, c)
+            x_q[(0, c)] = quantise(lo, E4M3, "x0_%d" % c)
+            x_q[(1, c)] = quantise(hi, E4M3, "x1_%d" % c)
+            g_quantise(0, c)
+            for h in range(2):
+                for t in range(TILES):
+                    mx_pass(t, h, c)
+
+        vector_block(1)
+        for h in range(2):
+            for t in range(TILES):
+                evacuate(t, h, nc.scalar.copy)
+                if h == 1:
+                    store(t)
+        for c in range(PASSES):
+            for h in range(2):
+                for t in range(TILES, 2 * TILES):
+                    mx_pass(t, h, c)
+        for c in range(PASSES):
+            g_copy_scalar(2, c)
+        vector_block(2)
+        for h in range(2):
+            for t in range(TILES, 2 * TILES):
+                evacuate(t, h, nc.scalar.copy)
+                if h == 1:
+                    store(t)
+
+        ahead = 0
+        for t in range(2 * TILES, 3 * TILES):
+            for h in range(2):
+                for c in range(PASSES):
+                    mx_pass(t, h, c)
+                if ahead < PASSES:
+                    g_copy_scalar(3, ahead)
+                    ahead += 1
+                evacuate(t, h, nc.scalar.copy)
+            store(t)
+        vector_block(3)
+
+        last = 4 * TILES - 1
+        for t in range(3 * TILES, 4 * TILES):
+            for h in range(2):
+                for c in range(PASSES):
+                    mx_pass(t, h, c)
+                if t == last:
+                    evacuate(t, h, nc.vector.tensor_copy if h == 0 else nc.scalar.copy)
+                    store_half(t, h)
+                else:
+                    evacuate(t, h, nc.scalar.copy)
+            if t != last:
+                store(t)

@@ -16,10 +16,9 @@ P = 128
 PACK = 4
 PASSES = 4
 UNIT = 512
-BLOCKS = 4
 TILES = 4
-S_COLS = (256, 0, 192, 192)
-PINNED = True
+S_COLS = (256, 0, 0, 192)
+SKEW = (1, 1, 2)
 
 
 def regroup(copy, grouped, source, col0, lo, hi):
@@ -37,27 +36,30 @@ def tile_primallinear_kernel(tc, x, weight, scale, grad_out, out):
         raw = ctx.enter_context(tc.tile_pool(name="raw", bufs=1))
         keep = ctx.enter_context(tc.tile_pool(name="keep", bufs=1))
         grp = ctx.enter_context(tc.tile_pool(name="grp", bufs=6))
-        stage = ctx.enter_context(tc.tile_pool(name="stage", bufs=8))
+        stage = ctx.enter_context(tc.tile_pool(name="stage", bufs=12))
         psum = ctx.enter_context(tc.psum_pool(name="psum", bufs=1))
-        if PINNED:
-            ctx.enter_context(tc.manual_schedule())
+        ctx.enter_context(tc.manual_schedule())
 
         x_raw = []
         g_raw = {}
 
-        def load_g(b, c):
-            t = raw.tile([P, PACK, UNIT], BF16, name="graw%d_%d" % (b, c))
-            nc.sync.dma_start(out=t[:], in_=gv[c, :, :, b * UNIT : (b + 1) * UNIT])
-            g_raw[(b, c)] = t
+        def load_g(c, first_block, blocks):
+            t = raw.tile([P, PACK, blocks * UNIT], BF16, name="graw%d_%d" % (first_block, c))
+            nc.sync.dma_start(
+                out=t[:], in_=gv[c, :, :, first_block * UNIT : (first_block + blocks) * UNIT]
+            )
+            for k in range(blocks):
+                g_raw[(first_block + k, c)] = (t, k * UNIT)
 
         for c in range(PASSES):
             t = raw.tile([P, PACK, 2 * UNIT], BF16, name="xraw%d" % c)
             nc.sync.dma_start(out=t[:], in_=xv[c, :, :, :])
             x_raw.append(t)
-            load_g(0, c)
-        for b in range(1, BLOCKS):
-            for c in range(PASSES):
-                load_g(b, c)
+            load_g(c, 0, 1)
+        for c in range(PASSES):
+            load_g(c, 1, 1)
+        for c in range(PASSES):
+            load_g(c, 2, 2)
 
         x_q = {}
         g_q = {}
@@ -83,11 +85,13 @@ def tile_primallinear_kernel(tc, x, weight, scale, grad_out, out):
             return g_grouped[(b, c)]
 
         def g_copy_vector(b, c):
-            regroup(nc.vector.tensor_copy, g_tile(b, c), g_raw[(b, c)], 0, 0, UNIT - S_COLS[b])
+            src, col0 = g_raw[(b, c)]
+            regroup(nc.vector.tensor_copy, g_tile(b, c), src, col0, 0, UNIT - S_COLS[b])
 
         def g_copy_scalar(b, c):
+            src, col0 = g_raw[(b, c)]
             if S_COLS[b] > 0:
-                regroup(nc.scalar.copy, g_tile(b, c), g_raw[(b, c)], 0, UNIT - S_COLS[b], UNIT)
+                regroup(nc.scalar.copy, g_tile(b, c), src, col0, UNIT - S_COLS[b], UNIT)
 
         def g_quantise(b, c):
             g_q[(b, c)] = quantise(g_tile(b, c), E5M2, "g%d_%d" % (b, c))
@@ -137,6 +141,19 @@ def tile_primallinear_kernel(tc, x, weight, scale, grad_out, out):
             g_quantise(b, 2)
             g_quantise(b, 3)
 
+        def streamed_passes(b):
+            order = sorted(
+                (SKEW[b] * j + 2 * TILES * c, j, c) for j in range(2 * TILES) for c in range(PASSES)
+            )
+            for key, j, c in order:
+                mx_pass(b * TILES + j // 2, j % 2, c)
+
+        def evacuate_block(b):
+            for t in range(b * TILES, (b + 1) * TILES):
+                evacuate(t, 0, nc.scalar.copy)
+                evacuate(t, 1, nc.scalar.copy)
+                store(t)
+
         for c in range(PASSES):
             lo = new_grouped()
             hi = new_grouped()
@@ -147,50 +164,31 @@ def tile_primallinear_kernel(tc, x, weight, scale, grad_out, out):
             x_q[(0, c)] = quantise(lo, E4M3, "x0_%d" % c)
             x_q[(1, c)] = quantise(hi, E4M3, "x1_%d" % c)
             g_quantise(0, c)
-            for h in range(2):
-                for t in range(TILES):
+            for t in range(TILES):
+                for h in range(2):
                     mx_pass(t, h, c)
 
         vector_block(1)
-        for h in range(2):
-            for t in range(TILES):
-                evacuate(t, h, nc.scalar.copy)
-                if h == 1:
-                    store(t)
-        for c in range(PASSES):
-            for h in range(2):
-                for t in range(TILES, 2 * TILES):
-                    mx_pass(t, h, c)
-        for c in range(PASSES):
-            g_copy_scalar(2, c)
-        vector_block(2)
-        for h in range(2):
-            for t in range(TILES, 2 * TILES):
-                evacuate(t, h, nc.scalar.copy)
-                if h == 1:
-                    store(t)
+        evacuate_block(0)
+        streamed_passes(1)
 
-        ahead = 0
-        for t in range(2 * TILES, 3 * TILES):
-            for h in range(2):
-                for c in range(PASSES):
-                    mx_pass(t, h, c)
-                if ahead < PASSES:
-                    g_copy_scalar(3, ahead)
-                    ahead += 1
-                evacuate(t, h, nc.scalar.copy)
-            store(t)
+        for c in range(PASSES):
+            g_copy_vector(2, c)
+            g_quantise(2, c)
+        evacuate_block(1)
+        streamed_passes(2)
+
+        for c in range(PASSES):
+            g_copy_scalar(3, c)
         vector_block(3)
-
+        evacuate_block(2)
         last = 4 * TILES - 1
         for t in range(3 * TILES, 4 * TILES):
             for h in range(2):
                 for c in range(PASSES):
                     mx_pass(t, h, c)
+                evacuate(t, h, nc.vector.tensor_copy if h == 0 else nc.scalar.copy)
                 if t == last:
-                    evacuate(t, h, nc.vector.tensor_copy if h == 0 else nc.scalar.copy)
                     store_half(t, h)
-                else:
-                    evacuate(t, h, nc.scalar.copy)
             if t != last:
                 store(t)

@@ -18,6 +18,7 @@ PASSES = 4
 UNIT = 512
 TILES = 4
 S_COLS = (256, 0, 0, 192)
+G_PAD = 48
 SKEW = (1, 1, 2)
 
 
@@ -36,7 +37,7 @@ def tile_primallinear_kernel(tc, x, weight, scale, grad_out, out):
         raw = ctx.enter_context(tc.tile_pool(name="raw", bufs=1))
         keep = ctx.enter_context(tc.tile_pool(name="keep", bufs=1))
         grp = ctx.enter_context(tc.tile_pool(name="grp", bufs=6))
-        stage = ctx.enter_context(tc.tile_pool(name="stage", bufs=12))
+        stage = ctx.enter_context(tc.tile_pool(name="stage", bufs=11))
         psum = ctx.enter_context(tc.psum_pool(name="psum", bufs=1))
         ctx.enter_context(tc.manual_schedule())
 
@@ -69,11 +70,12 @@ def tile_primallinear_kernel(tc, x, weight, scale, grad_out, out):
             t = grp.tile([P, UNIT, PACK], BF16, name="grouped", align_bytes=64)
             return t
 
-        def quantise(grouped, fmt, label):
-            codes = keep.tile([P, UNIT], U32, name="codes_" + label, align_bytes=64)
-            scales = keep.tile([P, UNIT], U8, name="scales_" + label, align_bytes=64)
+        def quantise(grouped, fmt, label, pad):
+            whole = keep.tile([P, pad + UNIT], U32, name="codes_" + label, align_bytes=256)
+            codes = whole[:, pad : pad + UNIT]
+            scales = keep.tile([P, UNIT], U8, name="scales_" + label, align_bytes=256)
             nc.vector.quantize_mx(
-                out=codes[:].bitcast(fmt),
+                out=codes.bitcast(fmt),
                 scales=scales[:],
                 in_=grouped[:].rearrange("p w t -> p (w t)"),
             )
@@ -94,7 +96,7 @@ def tile_primallinear_kernel(tc, x, weight, scale, grad_out, out):
                 regroup(nc.scalar.copy, g_tile(b, c), src, col0, UNIT - S_COLS[b], UNIT)
 
         def g_quantise(b, c):
-            g_q[(b, c)] = quantise(g_tile(b, c), E5M2, "g%d_%d" % (b, c))
+            g_q[(b, c)] = quantise(g_tile(b, c), E5M2, "g%d_%d" % (b, c), G_PAD)
 
         acc = {}
 
@@ -109,7 +111,7 @@ def tile_primallinear_kernel(tc, x, weight, scale, grad_out, out):
                 out=acc[(t, h)][:],
                 lhsT=codes[:, m0 : m0 + P].bitcast(E5M2),
                 lhsT_scale=scales[:, m0 : m0 + P],
-                rhs=xc[:].bitcast(E4M3),
+                rhs=xc.bitcast(E4M3),
                 rhs_scale=xs[:],
                 start=(c == 0),
                 stop=(c == PASSES - 1),
@@ -161,8 +163,8 @@ def tile_primallinear_kernel(tc, x, weight, scale, grad_out, out):
             regroup(nc.scalar.copy, hi, x_raw[c], UNIT, 0, UNIT)
             g_copy_vector(0, c)
             g_copy_scalar(0, c)
-            x_q[(0, c)] = quantise(lo, E4M3, "x0_%d" % c)
-            x_q[(1, c)] = quantise(hi, E4M3, "x1_%d" % c)
+            x_q[(0, c)] = quantise(lo, E4M3, "x0_%d" % c, 0)
+            x_q[(1, c)] = quantise(hi, E4M3, "x1_%d" % c, 0)
             g_quantise(0, c)
             for t in range(TILES):
                 for h in range(2):

@@ -15,182 +15,191 @@ E5M2 = mybir.dt.float8_e5m2_x4
 P = 128
 PACK = 4
 PASSES = 4
-UNIT = 512
+N = 512
+I = 1024
+BLOCK = 512
+HALF = 256
 TILES = 4
-S_COLS = (256, 0, 0, 192)
-G_PAD = 48
-SKEW = (1, 1, 2)
 
 
-def regroup(copy, grouped, source, col0, lo, hi):
+def regroup(copy, grouped, source, col0, first, past):
     copy(
-        out=grouped[:, lo:hi, :].rearrange("p (c i) t -> p c t i", i=4),
-        in_=source[:, :, col0 + lo : col0 + hi].rearrange("p t (c i) -> p c t i", i=4),
+        out=grouped[:, first:past, :].rearrange("p (c i) t -> p c t i", i=4),
+        in_=source[:, :, col0 + first : col0 + past].rearrange("p t (c i) -> p c t i", i=4),
     )
 
 
 def tile_primallinear_kernel(tc, x, weight, scale, grad_out, out):
     nc = tc.nc
+    vector = nc.vector.tensor_copy
+    scalar = nc.scalar.copy
     xv = x.rearrange("b (c p j) i -> (b c) p j i", p=P, j=PACK)
     gv = grad_out.rearrange("b (c p j) o -> (b c) p j o", p=P, j=PACK)
     with ExitStack() as ctx:
         raw = ctx.enter_context(tc.tile_pool(name="raw", bufs=1))
         keep = ctx.enter_context(tc.tile_pool(name="keep", bufs=1))
-        grp = ctx.enter_context(tc.tile_pool(name="grp", bufs=6))
+        xgrp = ctx.enter_context(tc.tile_pool(name="xgrp", bufs=3))
+        ggrp = ctx.enter_context(tc.tile_pool(name="ggrp", bufs=6))
         stage = ctx.enter_context(tc.tile_pool(name="stage", bufs=11))
         psum = ctx.enter_context(tc.psum_pool(name="psum", bufs=1))
         ctx.enter_context(tc.manual_schedule())
 
         x_raw = []
         g_raw = {}
-
-        def load_g(c, first_block, blocks):
-            t = raw.tile([P, PACK, blocks * UNIT], BF16, name="graw%d_%d" % (first_block, c))
-            nc.sync.dma_start(
-                out=t[:], in_=gv[c, :, :, first_block * UNIT : (first_block + blocks) * UNIT]
-            )
-            for k in range(blocks):
-                g_raw[(first_block + k, c)] = (t, k * UNIT)
-
         for c in range(PASSES):
-            t = raw.tile([P, PACK, 2 * UNIT], BF16, name="xraw%d" % c)
+            t = raw.tile([P, PACK, I], BF16, name="xraw%d" % c, tag="wide%d" % c)
             nc.sync.dma_start(out=t[:], in_=xv[c, :, :, :])
             x_raw.append(t)
-            load_g(c, 0, 1)
+            t = raw.tile([P, PACK, BLOCK], BF16, name="graw0_%d" % c)
+            nc.sync.dma_start(out=t[:], in_=gv[c, :, :, 0:BLOCK])
+            g_raw[(0, c)] = (t, 0)
         for c in range(PASSES):
-            load_g(c, 1, 1)
-        for c in range(PASSES):
-            load_g(c, 2, 2)
+            t = raw.tile([P, PACK, BLOCK], BF16, name="graw1_%d" % c)
+            nc.sync.dma_start(out=t[:], in_=gv[c, :, :, BLOCK : 2 * BLOCK])
+            g_raw[(1, c)] = (t, 0)
+
+        def load_last_blocks():
+            for c in range(PASSES):
+                t = raw.tile([P, PACK, 2 * BLOCK], BF16, name="graw23_%d" % c, tag="wide%d" % c)
+                nc.sync.dma_start(out=t[:], in_=gv[c, :, :, 2 * BLOCK : 4 * BLOCK])
+                g_raw[(2, c)] = (t, 0)
+                g_raw[(3, c)] = (t, BLOCK)
 
         x_q = {}
         g_q = {}
-        g_grouped = {}
+        grouped_of = {}
 
-        def new_grouped():
-            t = grp.tile([P, UNIT, PACK], BF16, name="grouped", align_bytes=64)
-            return t
-
-        def quantise(grouped, fmt, label, pad):
-            whole = keep.tile([P, pad + UNIT], U32, name="codes_" + label, align_bytes=256)
-            codes = whole[:, pad : pad + UNIT]
-            scales = keep.tile([P, UNIT], U8, name="scales_" + label, align_bytes=256)
+        def quantise(grouped, width, fmt, label):
+            codes = keep.tile([P, width], U32, name="codes_" + label, align_bytes=64)
+            scales = keep.tile([P, width], U8, name="scales_" + label, align_bytes=64)
             nc.vector.quantize_mx(
-                out=codes.bitcast(fmt),
+                out=codes[:].bitcast(fmt),
                 scales=scales[:],
                 in_=grouped[:].rearrange("p w t -> p (w t)"),
             )
             return codes, scales
 
-        def g_tile(b, c):
-            if (b, c) not in g_grouped:
-                g_grouped[(b, c)] = new_grouped()
-            return g_grouped[(b, c)]
+        def g_grouped(b, c, lo, width):
+            if (b, c, lo) not in grouped_of:
+                grouped_of[(b, c, lo)] = ggrp.tile(
+                    [P, width, PACK], BF16, name="grouped", align_bytes=64
+                )
+            return grouped_of[(b, c, lo)]
 
-        def g_copy_vector(b, c):
-            src, col0 = g_raw[(b, c)]
-            regroup(nc.vector.tensor_copy, g_tile(b, c), src, col0, 0, UNIT - S_COLS[b])
+        def g_regroup(copy, b, c, lo, width, first, past):
+            source, col0 = g_raw[(b, c)]
+            regroup(copy, g_grouped(b, c, lo, width), source, col0 + lo, first, past)
 
-        def g_copy_scalar(b, c):
-            src, col0 = g_raw[(b, c)]
-            if S_COLS[b] > 0:
-                regroup(nc.scalar.copy, g_tile(b, c), src, col0, UNIT - S_COLS[b], UNIT)
+        def g_quantise(b, c, lo, width):
+            codes, scales = quantise(
+                g_grouped(b, c, lo, width), width, E5M2, "g%d_%d_%d" % (b, c, lo)
+            )
+            for k in range(width // P):
+                g_q[(b * TILES + lo // P + k, c)] = (codes, scales, k * P)
 
-        def g_quantise(b, c):
-            g_q[(b, c)] = quantise(g_tile(b, c), E5M2, "g%d_%d" % (b, c), G_PAD)
+        def one_behind(copy_step, quantise_step):
+            copy_step(0)
+            for c in range(1, PASSES):
+                copy_step(c)
+                quantise_step(c - 1)
+            quantise_step(PASSES - 1)
 
         acc = {}
 
         def mx_pass(t, h, c):
             if c == 0:
-                bank = (t % TILES) * 2 + h
-                acc[(t, h)] = psum.tile([P, UNIT], F32, name="acc%d" % bank)
-            codes, scales = g_q[(t // TILES, c)]
-            m0 = (t % TILES) * P
-            xc, xs = x_q[(h, c)]
+                acc[(t, h)] = psum.tile([P, N], F32, name="acc%d" % ((t % TILES) * 2 + h))
+            codes, scales, m0 = g_q[(t, c)]
+            xc, xs = x_q[c]
             nc.tensor.matmul_mx(
                 out=acc[(t, h)][:],
                 lhsT=codes[:, m0 : m0 + P].bitcast(E5M2),
                 lhsT_scale=scales[:, m0 : m0 + P],
-                rhs=xc.bitcast(E4M3),
-                rhs_scale=xs[:],
+                rhs=xc[:, h * N : (h + 1) * N].bitcast(E4M3),
+                rhs_scale=xs[:, h * N : (h + 1) * N],
                 start=(c == 0),
                 stop=(c == PASSES - 1),
             )
+
+        def streamed(tiles, skew):
+            banks = [(t, h) for t in tiles for h in range(2)]
+            order = sorted(
+                (skew * j + len(banks) * c, j, c) for j in range(len(banks)) for c in range(PASSES)
+            )
+            for key, j, c in order:
+                mx_pass(banks[j][0], banks[j][1], c)
 
         staged = {}
 
         def evacuate(t, h, copy):
             if t not in staged:
-                staged[t] = stage.tile([P, 2 * UNIT], F32, name="staged")
-            copy(out=staged[t][:, h * UNIT : (h + 1) * UNIT], in_=acc[(t, h)][:])
+                staged[t] = stage.tile([P, I], F32, name="staged")
+            copy(out=staged[t][:, h * N : (h + 1) * N], in_=acc[(t, h)][:])
 
         def store(t):
             nc.sync.dma_start(out=out[t * P : (t + 1) * P, :], in_=staged[t][:])
 
         def store_half(t, h):
             nc.sync.dma_start(
-                out=out[t * P : (t + 1) * P, h * UNIT : (h + 1) * UNIT],
-                in_=staged[t][:, h * UNIT : (h + 1) * UNIT],
+                out=out[t * P : (t + 1) * P, h * N : (h + 1) * N],
+                in_=staged[t][:, h * N : (h + 1) * N],
             )
 
-        def vector_block(b):
-            g_copy_vector(b, 0)
-            g_copy_vector(b, 1)
-            g_quantise(b, 0)
-            g_copy_vector(b, 2)
-            g_quantise(b, 1)
-            g_copy_vector(b, 3)
-            g_quantise(b, 2)
-            g_quantise(b, 3)
-
-        def streamed_passes(b):
-            order = sorted(
-                (SKEW[b] * j + 2 * TILES * c, j, c) for j in range(2 * TILES) for c in range(PASSES)
-            )
-            for key, j, c in order:
-                mx_pass(b * TILES + j // 2, j % 2, c)
-
-        def evacuate_block(b):
-            for t in range(b * TILES, (b + 1) * TILES):
-                evacuate(t, 0, nc.scalar.copy)
-                evacuate(t, 1, nc.scalar.copy)
+        def drain(tiles, first_copy):
+            for t in tiles:
+                evacuate(t, 0, first_copy)
+                evacuate(t, 1, scalar)
                 store(t)
 
         for c in range(PASSES):
-            lo = new_grouped()
-            hi = new_grouped()
-            regroup(nc.vector.tensor_copy, lo, x_raw[c], 0, 0, UNIT)
-            regroup(nc.scalar.copy, hi, x_raw[c], UNIT, 0, UNIT)
-            g_copy_vector(0, c)
-            g_copy_scalar(0, c)
-            x_q[(0, c)] = quantise(lo, E4M3, "x0_%d" % c, 0)
-            x_q[(1, c)] = quantise(hi, E4M3, "x1_%d" % c, 0)
-            g_quantise(0, c)
+            xg = xgrp.tile([P, I, PACK], BF16, name="xgrouped", align_bytes=64)
+            regroup(vector, xg, x_raw[c], 0, 0, N)
+            regroup(scalar, xg, x_raw[c], 0, N, I)
+            g_regroup(vector, 0, c, 0, BLOCK, 0, HALF)
+            g_regroup(scalar, 0, c, 0, BLOCK, HALF, BLOCK)
+            x_q[c] = quantise(xg, I, E4M3, "x%d" % c)
+            g_quantise(0, c, 0, BLOCK)
             for t in range(TILES):
                 for h in range(2):
                     mx_pass(t, h, c)
+        load_last_blocks()
 
-        vector_block(1)
-        evacuate_block(0)
-        streamed_passes(1)
+        one_behind(
+            lambda c: g_regroup(vector, 1, c, 0, HALF, 0, HALF),
+            lambda c: g_quantise(1, c, 0, HALF),
+        )
+        g_regroup(scalar, 1, 0, HALF, HALF, 0, HALF)
+        drain([0, 1, 2, 3], scalar)
+        streamed([4, 5], 1)
+        g_regroup(scalar, 1, 3, HALF, HALF, 0, HALF)
+        g_regroup(vector, 1, 1, HALF, HALF, 0, HALF)
+        g_regroup(vector, 1, 2, HALF, HALF, 0, HALF)
+        for c in range(PASSES):
+            g_quantise(1, c, HALF, HALF)
+        drain([4, 5], scalar)
+        streamed([6, 7], 1)
 
         for c in range(PASSES):
-            g_copy_vector(2, c)
-            g_quantise(2, c)
-        evacuate_block(1)
-        streamed_passes(2)
+            g_regroup(vector, 2, c, 0, BLOCK, 0, BLOCK)
+            g_quantise(2, c, 0, BLOCK)
+        drain([6, 7], scalar)
+        streamed([8, 9, 10, 11], 2)
 
         for c in range(PASSES):
-            g_copy_scalar(3, c)
-        vector_block(3)
-        evacuate_block(2)
-        last = 4 * TILES - 1
-        for t in range(3 * TILES, 4 * TILES):
+            g_regroup(scalar, 3, c, 0, BLOCK, HALF, BLOCK)
+        one_behind(
+            lambda c: g_regroup(vector, 3, c, 0, BLOCK, 0, HALF),
+            lambda c: g_quantise(3, c, 0, BLOCK),
+        )
+        drain([8, 9, 10, 11], scalar)
+        streamed([12, 13], 1)
+        drain([12, 13], vector)
+        for t in (14, 15):
             for h in range(2):
                 for c in range(PASSES):
                     mx_pass(t, h, c)
-                evacuate(t, h, nc.vector.tensor_copy if h == 0 else nc.scalar.copy)
-                if t == last:
+                evacuate(t, h, vector if h == 0 else scalar)
+                if t == 15:
                     store_half(t, h)
-            if t != last:
+            if t == 14:
                 store(t)

from contextlib import ExitStack

import concourse.mybir as mybir

FLOPS = 2 * 2048 * 2048 * 1024
BYTES = 2 * 2048 * 1024 + 2 * 2048 * 2048 + 4 * 2048 * 1024

BF16 = mybir.dt.bfloat16
F32 = mybir.dt.float32
U32 = mybir.dt.uint32
U8 = mybir.dt.uint8
E4M3 = mybir.dt.float8_e4m3fn_x4
E5M2 = mybir.dt.float8_e5m2_x4

P = 128
PACK = 4
PASSES = 4
N = 512
I = 1024
BLOCK = 512
HALF = 256
TILES = 4


def regroup(copy, grouped, source, col0, first, past):
    copy(
        out=grouped[:, first:past, :].rearrange("p (c i) t -> p c t i", i=4),
        in_=source[:, :, col0 + first : col0 + past].rearrange("p t (c i) -> p c t i", i=4),
    )


def tile_primallinear_kernel(tc, x, weight, scale, grad_out, out):
    nc = tc.nc
    vector = nc.vector.tensor_copy
    scalar = nc.scalar.copy
    xv = x.rearrange("b (c p j) i -> (b c) p j i", p=P, j=PACK)
    gv = grad_out.rearrange("b (c p j) o -> (b c) p j o", p=P, j=PACK)
    with ExitStack() as ctx:
        raw = ctx.enter_context(tc.tile_pool(name="raw", bufs=1))
        keep = ctx.enter_context(tc.tile_pool(name="keep", bufs=1))
        xgrp = ctx.enter_context(tc.tile_pool(name="xgrp", bufs=3))
        ggrp = ctx.enter_context(tc.tile_pool(name="ggrp", bufs=6))
        stage = ctx.enter_context(tc.tile_pool(name="stage", bufs=11))
        psum = ctx.enter_context(tc.psum_pool(name="psum", bufs=1))
        ctx.enter_context(tc.manual_schedule())

        x_raw = []
        g_raw = {}
        for c in range(PASSES):
            t = raw.tile([P, PACK, I], BF16, name="xraw%d" % c, tag="wide%d" % c)
            nc.sync.dma_start(out=t[:], in_=xv[c, :, :, :])
            x_raw.append(t)
            t = raw.tile([P, PACK, BLOCK], BF16, name="graw0_%d" % c)
            nc.sync.dma_start(out=t[:], in_=gv[c, :, :, 0:BLOCK])
            g_raw[(0, c)] = (t, 0)
        for c in range(PASSES):
            t = raw.tile([P, PACK, BLOCK], BF16, name="graw1_%d" % c)
            nc.sync.dma_start(out=t[:], in_=gv[c, :, :, BLOCK : 2 * BLOCK])
            g_raw[(1, c)] = (t, 0)

        def load_last_blocks():
            for c in range(PASSES):
                t = raw.tile([P, PACK, 2 * BLOCK], BF16, name="graw23_%d" % c, tag="wide%d" % c)
                nc.sync.dma_start(out=t[:], in_=gv[c, :, :, 2 * BLOCK : 4 * BLOCK])
                g_raw[(2, c)] = (t, 0)
                g_raw[(3, c)] = (t, BLOCK)

        x_q = {}
        g_q = {}
        grouped_of = {}

        def quantise(grouped, width, fmt, label):
            codes = keep.tile([P, width], U32, name="codes_" + label, align_bytes=64)
            scales = keep.tile([P, width], U8, name="scales_" + label, align_bytes=64)
            nc.vector.quantize_mx(
                out=codes[:].bitcast(fmt),
                scales=scales[:],
                in_=grouped[:].rearrange("p w t -> p (w t)"),
            )
            return codes, scales

        def g_grouped(b, c, lo, width):
            if (b, c, lo) not in grouped_of:
                grouped_of[(b, c, lo)] = ggrp.tile(
                    [P, width, PACK], BF16, name="grouped", align_bytes=64
                )
            return grouped_of[(b, c, lo)]

        def g_regroup(copy, b, c, lo, width, first, past):
            source, col0 = g_raw[(b, c)]
            regroup(copy, g_grouped(b, c, lo, width), source, col0 + lo, first, past)

        def g_quantise(b, c, lo, width):
            codes, scales = quantise(
                g_grouped(b, c, lo, width), width, E5M2, "g%d_%d_%d" % (b, c, lo)
            )
            for k in range(width // P):
                g_q[(b * TILES + lo // P + k, c)] = (codes, scales, k * P)

        def one_behind(copy_step, quantise_step):
            copy_step(0)
            for c in range(1, PASSES):
                copy_step(c)
                quantise_step(c - 1)
            quantise_step(PASSES - 1)

        acc = {}

        def mx_pass(t, h, c):
            if c == 0:
                acc[(t, h)] = psum.tile([P, N], F32, name="acc%d" % ((t % TILES) * 2 + h))
            codes, scales, m0 = g_q[(t, c)]
            xc, xs = x_q[c]
            nc.tensor.matmul_mx(
                out=acc[(t, h)][:],
                lhsT=codes[:, m0 : m0 + P].bitcast(E5M2),
                lhsT_scale=scales[:, m0 : m0 + P],
                rhs=xc[:, h * N : (h + 1) * N].bitcast(E4M3),
                rhs_scale=xs[:, h * N : (h + 1) * N],
                start=(c == 0),
                stop=(c == PASSES - 1),
            )

        def streamed(tiles, skew):
            banks = [(t, h) for t in tiles for h in range(2)]
            order = sorted(
                (skew * j + len(banks) * c, j, c) for j in range(len(banks)) for c in range(PASSES)
            )
            for key, j, c in order:
                mx_pass(banks[j][0], banks[j][1], c)

        staged = {}

        def evacuate(t, h, copy):
            if t not in staged:
                staged[t] = stage.tile([P, I], F32, name="staged")
            copy(out=staged[t][:, h * N : (h + 1) * N], in_=acc[(t, h)][:])

        def store(t):
            nc.sync.dma_start(out=out[t * P : (t + 1) * P, :], in_=staged[t][:])

        def store_half(t, h):
            nc.sync.dma_start(
                out=out[t * P : (t + 1) * P, h * N : (h + 1) * N],
                in_=staged[t][:, h * N : (h + 1) * N],
            )

        def drain(tiles, first_copy):
            for t in tiles:
                evacuate(t, 0, first_copy)
                evacuate(t, 1, scalar)
                store(t)

        for c in range(PASSES):
            xg = xgrp.tile([P, I, PACK], BF16, name="xgrouped", align_bytes=64)
            regroup(vector, xg, x_raw[c], 0, 0, N)
            regroup(scalar, xg, x_raw[c], 0, N, I)
            g_regroup(vector, 0, c, 0, BLOCK, 0, HALF)
            g_regroup(scalar, 0, c, 0, BLOCK, HALF, BLOCK)
            x_q[c] = quantise(xg, I, E4M3, "x%d" % c)
            g_quantise(0, c, 0, BLOCK)
            for t in range(TILES):
                for h in range(2):
                    mx_pass(t, h, c)
        load_last_blocks()

        one_behind(
            lambda c: g_regroup(vector, 1, c, 0, HALF, 0, HALF),
            lambda c: g_quantise(1, c, 0, HALF),
        )
        g_regroup(scalar, 1, 0, HALF, HALF, 0, HALF)
        drain([0, 1, 2, 3], scalar)
        streamed([4, 5], 1)
        g_regroup(scalar, 1, 3, HALF, HALF, 0, HALF)
        g_regroup(vector, 1, 1, HALF, HALF, 0, HALF)
        g_regroup(vector, 1, 2, HALF, HALF, 0, HALF)
        for c in range(PASSES):
            g_quantise(1, c, HALF, HALF)
        drain([4, 5], scalar)
        streamed([6, 7], 1)

        for c in range(PASSES):
            g_regroup(vector, 2, c, 0, BLOCK, 0, BLOCK)
            g_quantise(2, c, 0, BLOCK)
        drain([6, 7], scalar)
        streamed([8, 9, 10, 11], 2)

        for c in range(PASSES):
            g_regroup(scalar, 3, c, 0, BLOCK, HALF, BLOCK)
        one_behind(
            lambda c: g_regroup(vector, 3, c, 0, BLOCK, 0, HALF),
            lambda c: g_quantise(3, c, 0, BLOCK),
        )
        drain([8, 9, 10, 11], scalar)
        streamed([12, 13], 1)
        drain([12, 13], vector)
        for t in (14, 15):
            for h in range(2):
                for c in range(PASSES):
                    mx_pass(t, h, c)
                evacuate(t, h, vector if h == 0 else scalar)
                if t == 15:
                    store_half(t, h)
            if t == 14:
                store(t)
